import numpy as np
import ml_dtypes


def mxq(x, axis, fmt="e4m3"):
    dtype, down = {"e4m3": (ml_dtypes.float8_e4m3fn, 7), "e5m2": (ml_dtypes.float8_e5m2, 14)}[fmt]
    v = np.moveaxis(np.asarray(x, np.float32).astype(ml_dtypes.bfloat16).astype(np.float64), axis, -1)
    blocks = v.reshape(v.shape[:-1] + (-1, 32))
    amax = np.abs(blocks).max(-1, keepdims=True)
    byte = np.maximum(np.where(amax > 0, np.frexp(amax)[1] - 1 + 127, 0) - down, 1)
    scale = np.exp2(byte - 127.0)
    codes = (blocks / scale).astype(np.float32).astype(dtype).astype(np.float64)
    return np.moveaxis((codes * scale).reshape(v.shape), -1, axis)


WIDE = False


def mx_kscale(k):
    if not WIDE:
        return np.ones(k)
    levels = np.array([10, -10, 5, -5, 0])
    if k % 512:
        return np.exp2(np.random.permutation(np.resize(levels, k // 32))).repeat(32)
    a = np.empty((k // 512, 16))
    for p in range(k // 512):
        a[p, :8] = np.random.permutation(np.resize(levels, 8))
        for g in range(8):
            far = levels[np.abs(levels - a[p, g]) >= 10]
            a[p, g + 8] = far[np.random.randint(len(far))]
    return np.exp2(a.ravel()).repeat(32)


BF16 = ml_dtypes.bfloat16


def bf(x):
    return np.asarray(x, np.float32).astype(BF16)


def f64(x):
    return np.asarray(x).astype(np.float64)


B, H, L, E, QD = 64, 1, 128, 1024, 128


def setup_inputs():
    s = mx_kscale(E)
    return {"x": bf(np.random.standard_normal((B, H, L, E)) * s),
            "Wk": bf(np.random.standard_normal((QD, E)) * 0.3 / np.sqrt(E) / s),
            "bk": bf(0.1 + 0.1 * np.random.standard_normal(QD)),
            "Wv": bf(np.random.standard_normal((QD, E)) * 0.3 / np.sqrt(E) / s),
            "bv": bf(0.1 + 0.1 * np.random.standard_normal(QD))}


def reference(x, Wk, bk, Wv, bv):
    xq = mxq(f64(x), 3, "e4m3")
    K = (xq @ mxq(f64(Wk), 1, "e4m3").T) + f64(bk)
    V = (xq @ mxq(f64(Wv), 1, "e4m3").T) + f64(bv)
    return K * V

@@ -1,0 +1,172 @@
+from contextlib import ExitStack
+
+import concourse.mybir as mybir
+from concourse.masks import make_identity
+
+BF16 = mybir.dt.bfloat16
+F32 = mybir.dt.float32
+U32 = mybir.dt.uint32
+U8 = mybir.dt.uint8
+FP8X4 = mybir.dt.float8_e4m3fn_x4
+ADD = mybir.AluOpType.add
+MULT = mybir.AluOpType.mult
+
+P = 128
+ROWS = 64 * 128
+K = 1024
+QD = 128
+PACK = 4
+PASSES = K // (P * PACK)
+WORDS = K // 2
+BLOCKS = WORDS // P
+BOTH = 2 * QD
+TILES = 4
+CHUNKS = ROWS // (P * TILES)
+PAIRS = TILES // 2
+AHEAD = 8
+OUT_BUFS = 8
+
+FLOPS = 2 * ROWS * K * BOTH
+
+
+def tile_parallelretention_pa_t_kernel(tc, x, Wk, bk, Wv, bv, out):
+    nc = tc.nc
+    x_pairs = x.flatten_outer_dims().rearrange("(c p h i) k -> c h p (i k)", c=CHUNKS, p=P, h=PAIRS, i=2)
+    out_chunks = out.flatten_outer_dims().rearrange("(c p j) q -> c p (j q)", c=CHUNKS, p=P, j=TILES)
+
+    with ExitStack() as ctx:
+        ctx.enter_context(tc.manual_schedule())
+        const = ctx.enter_context(tc.tile_pool(name="const", bufs=1))
+        x_pool = ctx.enter_context(tc.tile_pool(name="x_pool", bufs=AHEAD * PAIRS))
+        mx_pool = ctx.enter_context(tc.tile_pool(name="mx_pool", bufs=3))
+        out_pool = ctx.enter_context(tc.tile_pool(name="out_pool", bufs=OUT_BUFS))
+        turned_pool = ctx.enter_context(tc.psum_pool(name="turned_pool", bufs=TILES))
+        sums_pool = ctx.enter_context(tc.psum_pool(name="sums_pool", bufs=2 * PAIRS))
+
+        x_tiles = {}
+
+        def load_chunk(c):
+            for h in range(PAIRS):
+                x_tiles[c, h] = x_pool.tile([P, 2 * K], BF16, name="x_rows")
+                nc.sync.dma_start(out=x_tiles[c, h][:], in_=x_pairs[c, h])
+
+        def turn_row_tile(row_words, grouped_words):
+            turned = turned_pool.tile([P, WORDS], F32, name="turned")
+            for b in range(BLOCKS):
+                g, u = divmod(b, 2)
+                nc.tensor.transpose(
+                    out=turned[:, b * P : (b + 1) * P],
+                    in_=row_words[:, 2 * P * g + u : 2 * P * (g + 1) : 2],
+                    identity=identity[:],
+                )
+            nc.scalar.copy(
+                out=grouped_words,
+                in_=turned[:].rearrange("p (g u r) -> p g r u", g=PASSES, u=2),
+            )
+
+        identity = const.tile([P, P], F32, name="identity")
+        make_identity(nc, identity[:])
+
+        bias_rows = const.tile([P, BOTH], BF16, name="bias_rows")
+        nc.vector.memset(bias_rows[:], 0.0)
+        nc.scalar.dma_start(out=bias_rows[0:1, 0:QD], in_=bk.rearrange("(o q) -> o q", o=1))
+        nc.scalar.dma_start(out=bias_rows[0:1, QD:BOTH], in_=bv.rearrange("(o q) -> o q", o=1))
+        ones = const.tile([P, P], BF16, name="ones")
+        nc.vector.memset(ones[:], 1.0)
+
+        load_chunk(0)
+        w_rows = const.tile([P, 2 * K], BF16, name="w_rows")
+        nc.sync.dma_start(out=w_rows[:, 0:K], in_=Wk)
+        nc.sync.dma_start(out=w_rows[:, K : 2 * K], in_=Wv)
+        for c in range(1, AHEAD):
+            load_chunk(c)
+
+        grouped_tiles = {}
+        code_tiles = {}
+        scale_tiles = {}
+        sum_tiles = {}
+        biased_tiles = {}
+
+        def turn_chunk(c):
+            grouped_tiles[c] = mx_pool.tile([P, TILES * K], BF16, name="grouped", align_bytes=64)
+            code_tiles[c] = mx_pool.tile([P, TILES * K // PACK], U32, name="codes", align_bytes=64)
+            scale_tiles[c] = mx_pool.tile([P, TILES * K // PACK], U8, name="scales", align_bytes=64)
+            grouped_words = grouped_tiles[c][:].bitcast(F32)
+            for j in range(TILES):
+                h, i = divmod(j, 2)
+                turn_row_tile(
+                    x_tiles[c, h][:].bitcast(F32)[:, i * WORDS : (i + 1) * WORDS],
+                    grouped_words[:, j * WORDS : (j + 1) * WORDS].rearrange("p (g r u) -> p g r u", g=PASSES, u=2),
+                )
+
+        def quantise_pair(c, h):
+            width = 2 * K // PACK
+            nc.vector.quantize_mx(
+                out=code_tiles[c][:, h * width : (h + 1) * width].bitcast(FP8X4),
+                scales=scale_tiles[c][:, h * width : (h + 1) * width],
+                in_=grouped_tiles[c][:, h * width * PACK : (h + 1) * width * PACK],
+            )
+
+        def multiply_chunk(c):
+            for h in range(PAIRS):
+                sums = sums_pool.tile([P, 2 * BOTH], F32, name="sums")
+                sum_tiles[c, h] = sums
+                for i in range(2):
+                    for g in range(PASSES):
+                        first = ((2 * h + i) * PASSES + g) * P
+                        nc.tensor.matmul_mx(
+                            out=sums[:, i * BOTH : (i + 1) * BOTH],
+                            lhsT=code_tiles[c][:, first : first + P].bitcast(FP8X4),
+                            lhsT_scale=scale_tiles[c][:, first : first + P],
+                            rhs=w_codes[:, g * BOTH : (g + 1) * BOTH].bitcast(FP8X4),
+                            rhs_scale=w_scales[:, g * BOTH : (g + 1) * BOTH],
+                            start=(g == 0),
+                            stop=(g == PASSES - 1),
+                        )
+
+        def add_bias_pair(c, h):
+            if h == 0:
+                biased_tiles[c] = mx_pool.tile([P, TILES, BOTH], F32, name="biased")
+            nc.vector.tensor_tensor(
+                out=biased_tiles[c][:, 2 * h : 2 * h + 2, :],
+                in0=sum_tiles[c, h][:].rearrange("p (i n) -> p i n", i=2),
+                in1=bias[:].unsqueeze(1).to_broadcast([P, 2, BOTH]),
+                op=ADD,
+            )
+
+        def finish_chunk(c):
+            kv = out_pool.tile([P, TILES, QD], F32, name="kv")
+            nc.gpsimd.tensor_tensor(
+                out=kv[:], in0=biased_tiles[c][:, :, 0:QD], in1=biased_tiles[c][:, :, QD:BOTH], op=MULT
+            )
+            nc.sync.dma_start(out=out_chunks[c], in_=kv[:].rearrange("p j q -> p (j q)"))
+
+        turn_chunk(0)
+        for h in range(PAIRS):
+            quantise_pair(0, h)
+
+        w_grouped = const.tile([P, PASSES * BOTH * PACK], BF16, name="w_grouped", align_bytes=64)
+        w_codes = const.tile([P, PASSES * BOTH], U32, name="w_codes", align_bytes=64)
+        w_scales = const.tile([P, PASSES * BOTH], U8, name="w_scales", align_bytes=64)
+        w_words = w_rows[:].bitcast(F32)
+        w_grouped_words = w_grouped[:].bitcast(F32).rearrange("p (g v r u) -> p g v r u", g=PASSES, v=2, u=2)
+        for v in range(2):
+            turn_row_tile(w_words[:, v * WORDS : (v + 1) * WORDS], w_grouped_words[:, :, v, :, :])
+        nc.vector.quantize_mx(out=w_codes[:].bitcast(FP8X4), scales=w_scales[:], in_=w_grouped[:])
+
+        bias_sums = sums_pool.tile([P, 2 * BOTH], F32, name="sums")
+        nc.tensor.matmul(out=bias_sums[:, 0:BOTH], lhsT=ones[:], rhs=bias_rows[:], start=True, stop=True)
+        bias = const.tile([P, BOTH], F32, name="bias")
+        nc.vector.tensor_copy(out=bias[:], in_=bias_sums[:, 0:BOTH])
+
+        for c in range(1, CHUNKS + 1):
+            if c - 1 + AHEAD < CHUNKS:
+                load_chunk(c - 1 + AHEAD)
+            if c < CHUNKS:
+                turn_chunk(c)
+            multiply_chunk(c - 1)
+            for h in range(PAIRS):
+                if c < CHUNKS:
+                    quantise_pair(c, h)
+                add_bias_pair(c - 1, h)
+            finish_chunk(c - 1)

@@ -23,6 +23,8 @@ BOTH = 2 * QD
 TILES = 4
 CHUNKS = ROWS // (P * TILES)
 PAIRS = TILES // 2
+VECTOR_SORTS = 0
+SCALAR_SORTS = 2
 AHEAD = 8
 OUT_BUFS = 8
 
@@ -38,27 +40,40 @@ def tile_parallelretention_pa_t_kernel(tc, x, Wk, bk, Wv, bv, out):
         ctx.enter_context(tc.manual_schedule())
         const = ctx.enter_context(tc.tile_pool(name="const", bufs=1))
         x_pool = ctx.enter_context(tc.tile_pool(name="x_pool", bufs=AHEAD * PAIRS))
+        sort_pool = ctx.enter_context(tc.tile_pool(name="sort_pool", bufs=4))
         mx_pool = ctx.enter_context(tc.tile_pool(name="mx_pool", bufs=3))
         out_pool = ctx.enter_context(tc.tile_pool(name="out_pool", bufs=OUT_BUFS))
         turned_pool = ctx.enter_context(tc.psum_pool(name="turned_pool", bufs=TILES))
         sums_pool = ctx.enter_context(tc.psum_pool(name="sums_pool", bufs=2 * PAIRS))
 
         x_tiles = {}
+        sorted_tiles = {}
 
         def load_chunk(c):
             for h in range(PAIRS):
                 x_tiles[c, h] = x_pool.tile([P, 2 * K], BF16, name="x_rows")
                 nc.sync.dma_start(out=x_tiles[c, h][:], in_=x_pairs[c, h])
 
-        def turn_row_tile(row_words, grouped_words):
+        def sort_words(c, j):
+            h, i = divmod(j, 2)
+            sorted_tiles[c, j] = sort_pool.tile([P, K], BF16, name="sorted_%d" % j)
+            out_words = sorted_tiles[c, j][:].bitcast(F32).rearrange("p (g u m) -> p g u m", g=PASSES, u=2)
+            in_words = x_tiles[c, h][:].bitcast(F32)[:, i * WORDS : (i + 1) * WORDS]
+            in_words = in_words.rearrange("p (g m u) -> p g u m", g=PASSES, u=2)
+            if j == VECTOR_SORTS:
+                nc.vector.tensor_copy(out=out_words, in_=in_words)
+            else:
+                nc.scalar.copy(out=out_words, in_=in_words)
+
+        def turn_row_tile(row_words, grouped_words, is_sorted=False):
             turned = turned_pool.tile([P, WORDS], F32, name="turned")
             for b in range(BLOCKS):
                 g, u = divmod(b, 2)
-                nc.tensor.transpose(
-                    out=turned[:, b * P : (b + 1) * P],
-                    in_=row_words[:, 2 * P * g + u : 2 * P * (g + 1) : 2],
-                    identity=identity[:],
-                )
+                if is_sorted:
+                    block = row_words[:, b * P : (b + 1) * P]
+                else:
+                    block = row_words[:, 2 * P * g + u : 2 * P * (g + 1) : 2]
+                nc.tensor.transpose(out=turned[:, b * P : (b + 1) * P], in_=block, identity=identity[:])
             nc.scalar.copy(
                 out=grouped_words,
                 in_=turned[:].rearrange("p (g u r) -> p g r u", g=PASSES, u=2),
@@ -94,9 +109,15 @@ def tile_parallelretention_pa_t_kernel(tc, x, Wk, bk, Wv, bv, out):
             grouped_words = grouped_tiles[c][:].bitcast(F32)
             for j in range(TILES):
                 h, i = divmod(j, 2)
+                is_sorted = (c, j) in sorted_tiles
+                if is_sorted:
+                    row_words = sorted_tiles[c, j][:].bitcast(F32)
+                else:
+                    row_words = x_tiles[c, h][:].bitcast(F32)[:, i * WORDS : (i + 1) * WORDS]
                 turn_row_tile(
-                    x_tiles[c, h][:].bitcast(F32)[:, i * WORDS : (i + 1) * WORDS],
+                    row_words,
                     grouped_words[:, j * WORDS : (j + 1) * WORDS].rearrange("p (g r u) -> p g r u", g=PASSES, u=2),
+                    is_sorted,
                 )
 
         def quantise_pair(c, h):
@@ -159,14 +180,22 @@ def tile_parallelretention_pa_t_kernel(tc, x, Wk, bk, Wv, bv, out):
         bias = const.tile([P, BOTH], F32, name="bias")
         nc.vector.tensor_copy(out=bias[:], in_=bias_sums[:, 0:BOTH])
 
+        sort_words(1, VECTOR_SORTS)
+        sort_words(1, SCALAR_SORTS)
+        sort_words(2, VECTOR_SORTS)
+
         for c in range(1, CHUNKS + 1):
             if c - 1 + AHEAD < CHUNKS:
                 load_chunk(c - 1 + AHEAD)
             if c < CHUNKS:
                 turn_chunk(c)
             multiply_chunk(c - 1)
+            if c + 1 < CHUNKS:
+                sort_words(c + 1, SCALAR_SORTS)
             for h in range(PAIRS):
                 if c < CHUNKS:
                     quantise_pair(c, h)
                 add_bias_pair(c - 1, h)
+            if c + 2 < CHUNKS:
+                sort_words(c + 2, VECTOR_SORTS)
             finish_chunk(c - 1)

@@ -157,7 +157,7 @@ def tile_parallelretention_pa_t_kernel(tc, x, Wk, bk, Wv, bv, out):
 
         def finish_chunk(c):
             kv = out_pool.tile([P, TILES, QD], F32, name="kv")
-            nc.gpsimd.tensor_tensor(
+            nc.vector.tensor_tensor(
                 out=kv[:], in0=biased_tiles[c][:, :, 0:QD], in1=biased_tiles[c][:, :, QD:BOTH], op=MULT
             )
             nc.sync.dma_start(out=out_chunks[c], in_=kv[:].rearrange("p j q -> p (j q)"))
@@ -195,7 +195,9 @@ def tile_parallelretention_pa_t_kernel(tc, x, Wk, bk, Wv, bv, out):
             for h in range(PAIRS):
                 if c < CHUNKS:
                     quantise_pair(c, h)
+                if h == 1 and c + 2 < CHUNKS:
+                    sort_words(c + 2, VECTOR_SORTS)
                 add_bias_pair(c - 1, h)
-            if c + 2 < CHUNKS:
-                sort_words(c + 2, VECTOR_SORTS)
-            finish_chunk(c - 1)
+            if c > 1:
+                finish_chunk(c - 2)
+        finish_chunk(CHUNKS - 1)

@@ -120,13 +120,8 @@ def tile_parallelretention_pa_t_kernel(tc, x, Wk, bk, Wv, bv, out):
                     is_sorted,
                 )
 
-        def quantise_pair(c, h):
-            width = 2 * K // PACK
-            nc.vector.quantize_mx(
-                out=code_tiles[c][:, h * width : (h + 1) * width].bitcast(FP8X4),
-                scales=scale_tiles[c][:, h * width : (h + 1) * width],
-                in_=grouped_tiles[c][:, h * width * PACK : (h + 1) * width * PACK],
-            )
+        def quantise_chunk(c):
+            nc.vector.quantize_mx(out=code_tiles[c][:].bitcast(FP8X4), scales=scale_tiles[c][:], in_=grouped_tiles[c][:])
 
         def multiply_chunk(c):
             for h in range(PAIRS):
@@ -155,16 +150,15 @@ def tile_parallelretention_pa_t_kernel(tc, x, Wk, bk, Wv, bv, out):
                 op=ADD,
             )
 
-        def finish_chunk(c):
+        def finish_chunk(c, engine):
             kv = out_pool.tile([P, TILES, QD], F32, name="kv")
-            nc.vector.tensor_tensor(
+            engine.tensor_tensor(
                 out=kv[:], in0=biased_tiles[c][:, :, 0:QD], in1=biased_tiles[c][:, :, QD:BOTH], op=MULT
             )
             nc.sync.dma_start(out=out_chunks[c], in_=kv[:].rearrange("p j q -> p (j q)"))
 
         turn_chunk(0)
-        for h in range(PAIRS):
-            quantise_pair(0, h)
+        quantise_chunk(0)
 
         w_grouped = const.tile([P, PASSES * BOTH * PACK], BF16, name="w_grouped", align_bytes=64)
         w_codes = const.tile([P, PASSES * BOTH], U32, name="w_codes", align_bytes=64)
@@ -180,8 +174,6 @@ def tile_parallelretention_pa_t_kernel(tc, x, Wk, bk, Wv, bv, out):
         bias = const.tile([P, BOTH], F32, name="bias")
         nc.vector.tensor_copy(out=bias[:], in_=bias_sums[:, 0:BOTH])
 
-        sort_words(1, VECTOR_SORTS)
-        sort_words(1, SCALAR_SORTS)
         sort_words(2, VECTOR_SORTS)
 
         for c in range(1, CHUNKS + 1):
@@ -192,12 +184,14 @@ def tile_parallelretention_pa_t_kernel(tc, x, Wk, bk, Wv, bv, out):
             multiply_chunk(c - 1)
             if c + 1 < CHUNKS:
                 sort_words(c + 1, SCALAR_SORTS)
+            if c < CHUNKS:
+                quantise_chunk(c)
+                mark = mx_pool.tile([P, 1], U32, name="mark")
+                nc.gpsimd.tensor_copy(out=mark[:], in_=code_tiles[c][:, 0:1])
             for h in range(PAIRS):
-                if c < CHUNKS:
-                    quantise_pair(c, h)
-                if h == 1 and c + 2 < CHUNKS:
-                    sort_words(c + 2, VECTOR_SORTS)
                 add_bias_pair(c - 1, h)
             if c > 1:
-                finish_chunk(c - 2)
-        finish_chunk(CHUNKS - 1)
+                finish_chunk(c - 2, nc.gpsimd)
+            if c + 2 < CHUNKS:
+                sort_words(c + 2, VECTOR_SORTS)
+        finish_chunk(CHUNKS - 1, nc.vector)

@@ -23,7 +23,6 @@ BOTH = 2 * QD
 TILES = 4
 CHUNKS = ROWS // (P * TILES)
 PAIRS = TILES // 2
-VECTOR_SORTS = 0
 SCALAR_SORTS = 2
 AHEAD = 8
 OUT_BUFS = 8
@@ -60,10 +59,7 @@ def tile_parallelretention_pa_t_kernel(tc, x, Wk, bk, Wv, bv, out):
             out_words = sorted_tiles[c, j][:].bitcast(F32).rearrange("p (g u m) -> p g u m", g=PASSES, u=2)
             in_words = x_tiles[c, h][:].bitcast(F32)[:, i * WORDS : (i + 1) * WORDS]
             in_words = in_words.rearrange("p (g m u) -> p g u m", g=PASSES, u=2)
-            if j == VECTOR_SORTS:
-                nc.vector.tensor_copy(out=out_words, in_=in_words)
-            else:
-                nc.scalar.copy(out=out_words, in_=in_words)
+            nc.scalar.copy(out=out_words, in_=in_words)
 
         def turn_row_tile(row_words, grouped_words, is_sorted=False):
             turned = turned_pool.tile([P, WORDS], F32, name="turned")
@@ -150,9 +146,9 @@ def tile_parallelretention_pa_t_kernel(tc, x, Wk, bk, Wv, bv, out):
                 op=ADD,
             )
 
-        def finish_chunk(c, engine):
+        def finish_chunk(c):
             kv = out_pool.tile([P, TILES, QD], F32, name="kv")
-            engine.tensor_tensor(
+            nc.vector.tensor_tensor(
                 out=kv[:], in0=biased_tiles[c][:, :, 0:QD], in1=biased_tiles[c][:, :, QD:BOTH], op=MULT
             )
             nc.sync.dma_start(out=out_chunks[c], in_=kv[:].rearrange("p j q -> p (j q)"))
@@ -174,7 +170,6 @@ def tile_parallelretention_pa_t_kernel(tc, x, Wk, bk, Wv, bv, out):
         bias = const.tile([P, BOTH], F32, name="bias")
         nc.vector.tensor_copy(out=bias[:], in_=bias_sums[:, 0:BOTH])
 
-        sort_words(2, VECTOR_SORTS)
 
         for c in range(1, CHUNKS + 1):
             if c - 1 + AHEAD < CHUNKS:
@@ -186,12 +181,8 @@ def tile_parallelretention_pa_t_kernel(tc, x, Wk, bk, Wv, bv, out):
                 sort_words(c + 1, SCALAR_SORTS)
             if c < CHUNKS:
                 quantise_chunk(c)
-                mark = mx_pool.tile([P, 1], U32, name="mark")
-                nc.gpsimd.tensor_copy(out=mark[:], in_=code_tiles[c][:, 0:1])
             for h in range(PAIRS):
                 add_bias_pair(c - 1, h)
             if c > 1:
-                finish_chunk(c - 2, nc.gpsimd)
-            if c + 2 < CHUNKS:
-                sort_words(c + 2, VECTOR_SORTS)
-        finish_chunk(CHUNKS - 1, nc.vector)
+                finish_chunk(c - 2)
+        finish_chunk(CHUNKS - 1)

@@ -141,14 +141,14 @@ def tile_parallelretention_pa_t_kernel(tc, x, Wk, bk, Wv, bv, out):
                 biased_tiles[c] = mx_pool.tile([P, TILES, BOTH], F32, name="biased")
             nc.vector.tensor_tensor(
                 out=biased_tiles[c][:, 2 * h : 2 * h + 2, :],
-                in0=sum_tiles[c, h][:].rearrange("p (i n) -> p i n", i=2),
-                in1=bias[:].unsqueeze(1).to_broadcast([P, 2, BOTH]),
+                in0=bias[:].unsqueeze(1).to_broadcast([P, 2, BOTH]),
+                in1=sum_tiles[c, h][:].rearrange("p (i n) -> p i n", i=2),
                 op=ADD,
             )
 
-        def finish_chunk(c):
+        def finish_chunk(c, engine):
             kv = out_pool.tile([P, TILES, QD], F32, name="kv")
-            nc.vector.tensor_tensor(
+            engine.tensor_tensor(
                 out=kv[:], in0=biased_tiles[c][:, :, 0:QD], in1=biased_tiles[c][:, :, QD:BOTH], op=MULT
             )
             nc.sync.dma_start(out=out_chunks[c], in_=kv[:].rearrange("p j q -> p (j q)"))
@@ -181,8 +181,10 @@ def tile_parallelretention_pa_t_kernel(tc, x, Wk, bk, Wv, bv, out):
                 sort_words(c + 1, SCALAR_SORTS)
             if c < CHUNKS:
                 quantise_chunk(c)
+                mark = mx_pool.tile([P, 1], U32, name="mark")
+                nc.gpsimd.tensor_copy(out=mark[:], in_=code_tiles[c][:, 0:1])
             for h in range(PAIRS):
                 add_bias_pair(c - 1, h)
             if c > 1:
-                finish_chunk(c - 2)
-        finish_chunk(CHUNKS - 1)
+                finish_chunk(c - 2, nc.gpsimd)
+        finish_chunk(CHUNKS - 1, nc.vector)

@@ -23,7 +23,8 @@ BOTH = 2 * QD
 TILES = 4
 CHUNKS = ROWS // (P * TILES)
 PAIRS = TILES // 2
-SCALAR_SORTS = 2
+SORTED = (1, 2)
+VECTOR_COPY = 2
 AHEAD = 8
 OUT_BUFS = 8
 
@@ -48,10 +49,13 @@ def tile_parallelretention_pa_t_kernel(tc, x, Wk, bk, Wv, bv, out):
         x_tiles = {}
         sorted_tiles = {}
 
-        def load_chunk(c):
+        def load_chunk(c, pieces=1):
+            width = 2 * K // pieces
             for h in range(PAIRS):
                 x_tiles[c, h] = x_pool.tile([P, 2 * K], BF16, name="x_rows")
-                nc.sync.dma_start(out=x_tiles[c, h][:], in_=x_pairs[c, h])
+                for i in range(pieces):
+                    cols = slice(i * width, (i + 1) * width)
+                    nc.sync.dma_start(out=x_tiles[c, h][:, cols], in_=x_pairs[c, h][:, cols])
 
         def sort_words(c, j):
             h, i = divmod(j, 2)
@@ -61,7 +65,7 @@ def tile_parallelretention_pa_t_kernel(tc, x, Wk, bk, Wv, bv, out):
             in_words = in_words.rearrange("p (g m u) -> p g u m", g=PASSES, u=2)
             nc.scalar.copy(out=out_words, in_=in_words)
 
-        def turn_row_tile(row_words, grouped_words, is_sorted=False):
+        def turn_row_tile(row_words, grouped_words, is_sorted=False, on_vector=False):
             turned = turned_pool.tile([P, WORDS], F32, name="turned")
             for b in range(BLOCKS):
                 g, u = divmod(b, 2)
@@ -70,10 +74,8 @@ def tile_parallelretention_pa_t_kernel(tc, x, Wk, bk, Wv, bv, out):
                 else:
                     block = row_words[:, 2 * P * g + u : 2 * P * (g + 1) : 2]
                 nc.tensor.transpose(out=turned[:, b * P : (b + 1) * P], in_=block, identity=identity[:])
-            nc.scalar.copy(
-                out=grouped_words,
-                in_=turned[:].rearrange("p (g u r) -> p g r u", g=PASSES, u=2),
-            )
+            copy = nc.vector.tensor_copy if on_vector else nc.scalar.copy
+            copy(out=grouped_words, in_=turned[:].rearrange("p (g u r) -> p g r u", g=PASSES, u=2))
 
         identity = const.tile([P, P], F32, name="identity")
         make_identity(nc, identity[:])
@@ -85,7 +87,7 @@ def tile_parallelretention_pa_t_kernel(tc, x, Wk, bk, Wv, bv, out):
         ones = const.tile([P, P], BF16, name="ones")
         nc.vector.memset(ones[:], 1.0)
 
-        load_chunk(0)
+        load_chunk(0, pieces=2)
         w_rows = const.tile([P, 2 * K], BF16, name="w_rows")
         nc.sync.dma_start(out=w_rows[:, 0:K], in_=Wk)
         nc.sync.dma_start(out=w_rows[:, K : 2 * K], in_=Wv)
@@ -114,7 +116,18 @@ def tile_parallelretention_pa_t_kernel(tc, x, Wk, bk, Wv, bv, out):
                     row_words,
                     grouped_words[:, j * WORDS : (j + 1) * WORDS].rearrange("p (g r u) -> p g r u", g=PASSES, u=2),
                     is_sorted,
+                    on_vector=(c > 0 and j == VECTOR_COPY),
                 )
+                if c == 0 and j % 2 == 1:
+                    quantise_pair(c, h)
+
+        def quantise_pair(c, h):
+            width = 2 * K // PACK
+            nc.vector.quantize_mx(
+                out=code_tiles[c][:, h * width : (h + 1) * width].bitcast(FP8X4),
+                scales=scale_tiles[c][:, h * width : (h + 1) * width],
+                in_=grouped_tiles[c][:, h * width * PACK : (h + 1) * width * PACK],
+            )
 
         def quantise_chunk(c):
             nc.vector.quantize_mx(out=code_tiles[c][:].bitcast(FP8X4), scales=scale_tiles[c][:], in_=grouped_tiles[c][:])
@@ -146,15 +159,23 @@ def tile_parallelretention_pa_t_kernel(tc, x, Wk, bk, Wv, bv, out):
                 op=ADD,
             )
 
-        def finish_chunk(c, engine):
+        def finish_chunk(c, engine, pieces=1):
             kv = out_pool.tile([P, TILES, QD], F32, name="kv")
-            engine.tensor_tensor(
-                out=kv[:], in0=biased_tiles[c][:, :, 0:QD], in1=biased_tiles[c][:, :, QD:BOTH], op=MULT
-            )
-            nc.sync.dma_start(out=out_chunks[c], in_=kv[:].rearrange("p j q -> p (j q)"))
+            width = TILES // pieces
+            for i in range(pieces):
+                tiles = slice(i * width, (i + 1) * width)
+                engine.tensor_tensor(
+                    out=kv[:, tiles, :],
+                    in0=biased_tiles[c][:, tiles, 0:QD],
+                    in1=biased_tiles[c][:, tiles, QD:BOTH],
+                    op=MULT,
+                )
+                nc.sync.dma_start(
+                    out=out_chunks[c][:, i * width * QD : (i + 1) * width * QD],
+                    in_=kv[:, tiles, :].rearrange("p j q -> p (j q)"),
+                )
 
         turn_chunk(0)
-        quantise_chunk(0)
 
         w_grouped = const.tile([P, PASSES * BOTH * PACK], BF16, name="w_grouped", align_bytes=64)
         w_codes = const.tile([P, PASSES * BOTH], U32, name="w_codes", align_bytes=64)
@@ -170,21 +191,32 @@ def tile_parallelretention_pa_t_kernel(tc, x, Wk, bk, Wv, bv, out):
         bias = const.tile([P, BOTH], F32, name="bias")
         nc.vector.tensor_copy(out=bias[:], in_=bias_sums[:, 0:BOTH])
 
-
-        for c in range(1, CHUNKS + 1):
+        for c in range(1, CHUNKS):
             if c - 1 + AHEAD < CHUNKS:
                 load_chunk(c - 1 + AHEAD)
-            if c < CHUNKS:
-                turn_chunk(c)
+            if c > 1:
+                quantise_chunk(c - 1)
+                mark = mx_pool.tile([P, 1], U32, name="mark")
+                nc.gpsimd.tensor_copy(out=mark[:], in_=code_tiles[c - 1][:, 0:1])
+                add_bias_pair(c - 2, 0)
+            turn_chunk(c)
+            if c > 1:
+                add_bias_pair(c - 2, 1)
             multiply_chunk(c - 1)
             if c + 1 < CHUNKS:
-                sort_words(c + 1, SCALAR_SORTS)
-            if c < CHUNKS:
-                quantise_chunk(c)
-                mark = mx_pool.tile([P, 1], U32, name="mark")
-                nc.gpsimd.tensor_copy(out=mark[:], in_=code_tiles[c][:, 0:1])
-            for h in range(PAIRS):
-                add_bias_pair(c - 1, h)
-            if c > 1:
-                finish_chunk(c - 2, nc.gpsimd)
-        finish_chunk(CHUNKS - 1, nc.vector)
+                for j in SORTED:
+                    sort_words(c + 1, j)
+            if c > 2:
+                finish_chunk(c - 3, nc.gpsimd)
+
+        last = CHUNKS - 1
+        quantise_pair(last, 0)
+        add_bias_pair(last - 1, 0)
+        finish_chunk(last - 2, nc.gpsimd)
+        add_bias_pair(last - 1, 1)
+        quantise_pair(last, 1)
+        multiply_chunk(last)
+        finish_chunk(last - 1, nc.gpsimd)
+        for h in range(PAIRS):
+            add_bias_pair(last, h)
+        finish_chunk(last, nc.vector, pieces=PAIRS)

@@ -60,9 +60,9 @@ def tile_parallelretention_pa_t_kernel(tc, x, Wk, bk, Wv, bv, out):
         def sort_words(c, j):
             h, i = divmod(j, 2)
             sorted_tiles[c, j] = sort_pool.tile([P, K], BF16, name="sorted_%d" % j)
-            out_words = sorted_tiles[c, j][:].bitcast(F32).rearrange("p (g u m) -> p g u m", g=PASSES, u=2)
+            out_words = sorted_tiles[c, j][:].bitcast(F32).rearrange("p (g u m) -> p g m u", g=PASSES, u=2)
             in_words = x_tiles[c, h][:].bitcast(F32)[:, i * WORDS : (i + 1) * WORDS]
-            in_words = in_words.rearrange("p (g m u) -> p g u m", g=PASSES, u=2)
+            in_words = in_words.rearrange("p (g m u) -> p g m u", g=PASSES, u=2)
             nc.scalar.copy(out=out_words, in_=in_words)
 
         def turn_row_tile(row_words, grouped_words, is_sorted=False, on_vector=False):

@@ -26,7 +26,6 @@ PAIRS = TILES // 2
 SORTED = (1, 2)
 VECTOR_COPY = 2
 AHEAD = 8
-OUT_BUFS = 8
 
 FLOPS = 2 * ROWS * K * BOTH
 
@@ -41,8 +40,8 @@ def tile_parallelretention_pa_t_kernel(tc, x, Wk, bk, Wv, bv, out):
         const = ctx.enter_context(tc.tile_pool(name="const", bufs=1))
         x_pool = ctx.enter_context(tc.tile_pool(name="x_pool", bufs=AHEAD * PAIRS))
         sort_pool = ctx.enter_context(tc.tile_pool(name="sort_pool", bufs=4))
+        group_pool = ctx.enter_context(tc.tile_pool(name="group_pool", bufs=4))
         mx_pool = ctx.enter_context(tc.tile_pool(name="mx_pool", bufs=3))
-        out_pool = ctx.enter_context(tc.tile_pool(name="out_pool", bufs=OUT_BUFS))
         turned_pool = ctx.enter_context(tc.psum_pool(name="turned_pool", bufs=TILES))
         sums_pool = ctx.enter_context(tc.psum_pool(name="sums_pool", bufs=2 * PAIRS))
 
@@ -60,9 +59,9 @@ def tile_parallelretention_pa_t_kernel(tc, x, Wk, bk, Wv, bv, out):
         def sort_words(c, j):
             h, i = divmod(j, 2)
             sorted_tiles[c, j] = sort_pool.tile([P, K], BF16, name="sorted_%d" % j)
-            out_words = sorted_tiles[c, j][:].bitcast(F32).rearrange("p (g u m) -> p g m u", g=PASSES, u=2)
+            out_words = sorted_tiles[c, j][:].bitcast(F32).rearrange("p (u a b) -> p a u b", u=2, b=2)
             in_words = x_tiles[c, h][:].bitcast(F32)[:, i * WORDS : (i + 1) * WORDS]
-            in_words = in_words.rearrange("p (g m u) -> p g m u", g=PASSES, u=2)
+            in_words = in_words.rearrange("p (a b u) -> p a u b", u=2, b=2)
             nc.scalar.copy(out=out_words, in_=in_words)
 
         def turn_row_tile(row_words, grouped_words, is_sorted=False, on_vector=False):
@@ -70,7 +69,7 @@ def tile_parallelretention_pa_t_kernel(tc, x, Wk, bk, Wv, bv, out):
             for b in range(BLOCKS):
                 g, u = divmod(b, 2)
                 if is_sorted:
-                    block = row_words[:, b * P : (b + 1) * P]
+                    block = row_words[:, (2 * u + g) * P : (2 * u + g + 1) * P]
                 else:
                     block = row_words[:, 2 * P * g + u : 2 * P * (g + 1) : 2]
                 nc.tensor.transpose(out=turned[:, b * P : (b + 1) * P], in_=block, identity=identity[:])
@@ -101,7 +100,7 @@ def tile_parallelretention_pa_t_kernel(tc, x, Wk, bk, Wv, bv, out):
         biased_tiles = {}
 
         def turn_chunk(c):
-            grouped_tiles[c] = mx_pool.tile([P, TILES * K], BF16, name="grouped", align_bytes=64)
+            grouped_tiles[c] = group_pool.tile([P, TILES * K], BF16, name="grouped", align_bytes=64)
             code_tiles[c] = mx_pool.tile([P, TILES * K // PACK], U32, name="codes", align_bytes=64)
             scale_tiles[c] = mx_pool.tile([P, TILES * K // PACK], U8, name="scales", align_bytes=64)
             grouped_words = grouped_tiles[c][:].bitcast(F32)
@@ -159,8 +158,8 @@ def tile_parallelretention_pa_t_kernel(tc, x, Wk, bk, Wv, bv, out):
                 op=ADD,
             )
 
-        def finish_chunk(c, engine, pieces=1):
-            kv = out_pool.tile([P, TILES, QD], F32, name="kv")
+        def finish_chunk(c, engine, kv, pieces=1):
+            kv = kv.rearrange("p (j q) -> p j q", j=TILES)
             width = TILES // pieces
             for i in range(pieces):
                 tiles = slice(i * width, (i + 1) * width)
@@ -196,8 +195,6 @@ def tile_parallelretention_pa_t_kernel(tc, x, Wk, bk, Wv, bv, out):
                 load_chunk(c - 1 + AHEAD)
             if c > 1:
                 quantise_chunk(c - 1)
-                mark = mx_pool.tile([P, 1], U32, name="mark")
-                nc.gpsimd.tensor_copy(out=mark[:], in_=code_tiles[c - 1][:, 0:1])
                 add_bias_pair(c - 2, 0)
             turn_chunk(c)
             if c > 1:
@@ -207,16 +204,19 @@ def tile_parallelretention_pa_t_kernel(tc, x, Wk, bk, Wv, bv, out):
                 for j in SORTED:
                     sort_words(c + 1, j)
             if c > 2:
-                finish_chunk(c - 3, nc.gpsimd)
+                finish_chunk(c - 3, nc.gpsimd, grouped_tiles[c - 1][:].bitcast(F32)[:, 0 : TILES * QD])
 
         last = CHUNKS - 1
+        kv_before = const.tile([P, TILES * QD], F32, name="kv_before")
+        kv_next = const.tile([P, TILES * QD], F32, name="kv_next")
+        kv_last = const.tile([P, TILES * QD], F32, name="kv_last")
         quantise_pair(last, 0)
         add_bias_pair(last - 1, 0)
-        finish_chunk(last - 2, nc.gpsimd)
+        finish_chunk(last - 2, nc.gpsimd, kv_before[:])
         add_bias_pair(last - 1, 1)
         quantise_pair(last, 1)
         multiply_chunk(last)
-        finish_chunk(last - 1, nc.gpsimd)
+        finish_chunk(last - 1, nc.gpsimd, kv_next[:])
         for h in range(PAIRS):
             add_bias_pair(last, h)
-        finish_chunk(last, nc.vector, pieces=PAIRS)
+        finish_chunk(last, nc.vector, kv_last[:], pieces=PAIRS)

@@ -23,7 +23,7 @@ BOTH = 2 * QD
 TILES = 4
 CHUNKS = ROWS // (P * TILES)
 PAIRS = TILES // 2
-SORTED = (1, 2)
+SORTED = ((3,), (2, 3))
 VECTOR_COPY = 2
 AHEAD = 8
 
@@ -40,7 +40,7 @@ def tile_parallelretention_pa_t_kernel(tc, x, Wk, bk, Wv, bv, out):
         const = ctx.enter_context(tc.tile_pool(name="const", bufs=1))
         x_pool = ctx.enter_context(tc.tile_pool(name="x_pool", bufs=AHEAD * PAIRS))
         sort_pool = ctx.enter_context(tc.tile_pool(name="sort_pool", bufs=4))
-        group_pool = ctx.enter_context(tc.tile_pool(name="group_pool", bufs=4))
+        group_pool = ctx.enter_context(tc.tile_pool(name="group_pool", bufs=8))
         mx_pool = ctx.enter_context(tc.tile_pool(name="mx_pool", bufs=3))
         turned_pool = ctx.enter_context(tc.psum_pool(name="turned_pool", bufs=TILES))
         sums_pool = ctx.enter_context(tc.psum_pool(name="sums_pool", bufs=2 * PAIRS))
@@ -201,7 +201,7 @@ def tile_parallelretention_pa_t_kernel(tc, x, Wk, bk, Wv, bv, out):
                 add_bias_pair(c - 2, 1)
             multiply_chunk(c - 1)
             if c + 1 < CHUNKS:
-                for j in SORTED:
+                for j in SORTED[(c + 1) % 2]:
                     sort_words(c + 1, j)
             if c > 2:
                 finish_chunk(c - 3, nc.gpsimd, grouped_tiles[c - 1][:].bitcast(F32)[:, 0 : TILES * QD])

from contextlib import ExitStack

import concourse.mybir as mybir
from concourse.masks import make_identity

BF16 = mybir.dt.bfloat16
F32 = mybir.dt.float32
U32 = mybir.dt.uint32
U8 = mybir.dt.uint8
FP8X4 = mybir.dt.float8_e4m3fn_x4
ADD = mybir.AluOpType.add
MULT = mybir.AluOpType.mult

P = 128
ROWS = 64 * 128
K = 1024
QD = 128
PACK = 4
PASSES = K // (P * PACK)
WORDS = K // 2
BLOCKS = WORDS // P
BOTH = 2 * QD
TILES = 4
CHUNKS = ROWS // (P * TILES)
PAIRS = TILES // 2
SORTED = ((3,), (2, 3))
VECTOR_COPY = 2
AHEAD = 8

FLOPS = 2 * ROWS * K * BOTH


def tile_parallelretention_pa_t_kernel(tc, x, Wk, bk, Wv, bv, out):
    nc = tc.nc
    x_pairs = x.flatten_outer_dims().rearrange("(c p h i) k -> c h p (i k)", c=CHUNKS, p=P, h=PAIRS, i=2)
    out_chunks = out.flatten_outer_dims().rearrange("(c p j) q -> c p (j q)", c=CHUNKS, p=P, j=TILES)

    with ExitStack() as ctx:
        ctx.enter_context(tc.manual_schedule())
        const = ctx.enter_context(tc.tile_pool(name="const", bufs=1))
        x_pool = ctx.enter_context(tc.tile_pool(name="x_pool", bufs=AHEAD * PAIRS))
        sort_pool = ctx.enter_context(tc.tile_pool(name="sort_pool", bufs=4))
        group_pool = ctx.enter_context(tc.tile_pool(name="group_pool", bufs=8))
        mx_pool = ctx.enter_context(tc.tile_pool(name="mx_pool", bufs=3))
        turned_pool = ctx.enter_context(tc.psum_pool(name="turned_pool", bufs=TILES))
        sums_pool = ctx.enter_context(tc.psum_pool(name="sums_pool", bufs=2 * PAIRS))

        x_tiles = {}
        sorted_tiles = {}

        def load_chunk(c, pieces=1):
            width = 2 * K // pieces
            for h in range(PAIRS):
                x_tiles[c, h] = x_pool.tile([P, 2 * K], BF16, name="x_rows")
                for i in range(pieces):
                    cols = slice(i * width, (i + 1) * width)
                    nc.sync.dma_start(out=x_tiles[c, h][:, cols], in_=x_pairs[c, h][:, cols])

        def sort_words(c, j):
            h, i = divmod(j, 2)
            sorted_tiles[c, j] = sort_pool.tile([P, K], BF16, name="sorted_%d" % j)
            out_words = sorted_tiles[c, j][:].bitcast(F32).rearrange("p (u a b) -> p a u b", u=2, b=2)
            in_words = x_tiles[c, h][:].bitcast(F32)[:, i * WORDS : (i + 1) * WORDS]
            in_words = in_words.rearrange("p (a b u) -> p a u b", u=2, b=2)
            nc.scalar.copy(out=out_words, in_=in_words)

        def turn_row_tile(row_words, grouped_words, is_sorted=False, on_vector=False):
            turned = turned_pool.tile([P, WORDS], F32, name="turned")
            for b in range(BLOCKS):
                g, u = divmod(b, 2)
                if is_sorted:
                    block = row_words[:, (2 * u + g) * P : (2 * u + g + 1) * P]
                else:
                    block = row_words[:, 2 * P * g + u : 2 * P * (g + 1) : 2]
                nc.tensor.transpose(out=turned[:, b * P : (b + 1) * P], in_=block, identity=identity[:])
            copy = nc.vector.tensor_copy if on_vector else nc.scalar.copy
            copy(out=grouped_words, in_=turned[:].rearrange("p (g u r) -> p g r u", g=PASSES, u=2))

        identity = const.tile([P, P], F32, name="identity")
        make_identity(nc, identity[:])

        bias_rows = const.tile([P, BOTH], BF16, name="bias_rows")
        nc.vector.memset(bias_rows[:], 0.0)
        nc.scalar.dma_start(out=bias_rows[0:1, 0:QD], in_=bk.rearrange("(o q) -> o q", o=1))
        nc.scalar.dma_start(out=bias_rows[0:1, QD:BOTH], in_=bv.rearrange("(o q) -> o q", o=1))
        ones = const.tile([P, P], BF16, name="ones")
        nc.vector.memset(ones[:], 1.0)

        load_chunk(0, pieces=2)
        w_rows = const.tile([P, 2 * K], BF16, name="w_rows")
        nc.sync.dma_start(out=w_rows[:, 0:K], in_=Wk)
        nc.sync.dma_start(out=w_rows[:, K : 2 * K], in_=Wv)
        for c in range(1, AHEAD):
            load_chunk(c)

        grouped_tiles = {}
        code_tiles = {}
        scale_tiles = {}
        sum_tiles = {}
        biased_tiles = {}

        def turn_chunk(c):
            grouped_tiles[c] = group_pool.tile([P, TILES * K], BF16, name="grouped", align_bytes=64)
            code_tiles[c] = mx_pool.tile([P, TILES * K // PACK], U32, name="codes", align_bytes=64)
            scale_tiles[c] = mx_pool.tile([P, TILES * K // PACK], U8, name="scales", align_bytes=64)
            grouped_words = grouped_tiles[c][:].bitcast(F32)
            for j in range(TILES):
                h, i = divmod(j, 2)
                is_sorted = (c, j) in sorted_tiles
                if is_sorted:
                    row_words = sorted_tiles[c, j][:].bitcast(F32)
                else:
                    row_words = x_tiles[c, h][:].bitcast(F32)[:, i * WORDS : (i + 1) * WORDS]
                turn_row_tile(
                    row_words,
                    grouped_words[:, j * WORDS : (j + 1) * WORDS].rearrange("p (g r u) -> p g r u", g=PASSES, u=2),
                    is_sorted,
                    on_vector=(c > 0 and j == VECTOR_COPY),
                )
                if c == 0 and j % 2 == 1:
                    quantise_pair(c, h)

        def quantise_pair(c, h):
            width = 2 * K // PACK
            nc.vector.quantize_mx(
                out=code_tiles[c][:, h * width : (h + 1) * width].bitcast(FP8X4),
                scales=scale_tiles[c][:, h * width : (h + 1) * width],
                in_=grouped_tiles[c][:, h * width * PACK : (h + 1) * width * PACK],
            )

        def quantise_chunk(c):
            nc.vector.quantize_mx(out=code_tiles[c][:].bitcast(FP8X4), scales=scale_tiles[c][:], in_=grouped_tiles[c][:])

        def multiply_chunk(c):
            for h in range(PAIRS):
                sums = sums_pool.tile([P, 2 * BOTH], F32, name="sums")
                sum_tiles[c, h] = sums
                for i in range(2):
                    for g in range(PASSES):
                        first = ((2 * h + i) * PASSES + g) * P
                        nc.tensor.matmul_mx(
                            out=sums[:, i * BOTH : (i + 1) * BOTH],
                            lhsT=code_tiles[c][:, first : first + P].bitcast(FP8X4),
                            lhsT_scale=scale_tiles[c][:, first : first + P],
                            rhs=w_codes[:, g * BOTH : (g + 1) * BOTH].bitcast(FP8X4),
                            rhs_scale=w_scales[:, g * BOTH : (g + 1) * BOTH],
                            start=(g == 0),
                            stop=(g == PASSES - 1),
                        )

        def add_bias_pair(c, h):
            if h == 0:
                biased_tiles[c] = mx_pool.tile([P, TILES, BOTH], F32, name="biased")
            nc.vector.tensor_tensor(
                out=biased_tiles[c][:, 2 * h : 2 * h + 2, :],
                in0=bias[:].unsqueeze(1).to_broadcast([P, 2, BOTH]),
                in1=sum_tiles[c, h][:].rearrange("p (i n) -> p i n", i=2),
                op=ADD,
            )

        def finish_chunk(c, engine, kv, pieces=1):
            kv = kv.rearrange("p (j q) -> p j q", j=TILES)
            width = TILES // pieces
            for i in range(pieces):
                tiles = slice(i * width, (i + 1) * width)
                engine.tensor_tensor(
                    out=kv[:, tiles, :],
                    in0=biased_tiles[c][:, tiles, 0:QD],
                    in1=biased_tiles[c][:, tiles, QD:BOTH],
                    op=MULT,
                )
                nc.sync.dma_start(
                    out=out_chunks[c][:, i * width * QD : (i + 1) * width * QD],
                    in_=kv[:, tiles, :].rearrange("p j q -> p (j q)"),
                )

        turn_chunk(0)

        w_grouped = const.tile([P, PASSES * BOTH * PACK], BF16, name="w_grouped", align_bytes=64)
        w_codes = const.tile([P, PASSES * BOTH], U32, name="w_codes", align_bytes=64)
        w_scales = const.tile([P, PASSES * BOTH], U8, name="w_scales", align_bytes=64)
        w_words = w_rows[:].bitcast(F32)
        w_grouped_words = w_grouped[:].bitcast(F32).rearrange("p (g v r u) -> p g v r u", g=PASSES, v=2, u=2)
        for v in range(2):
            turn_row_tile(w_words[:, v * WORDS : (v + 1) * WORDS], w_grouped_words[:, :, v, :, :])
        nc.vector.quantize_mx(out=w_codes[:].bitcast(FP8X4), scales=w_scales[:], in_=w_grouped[:])

        bias_sums = sums_pool.tile([P, 2 * BOTH], F32, name="sums")
        nc.tensor.matmul(out=bias_sums[:, 0:BOTH], lhsT=ones[:], rhs=bias_rows[:], start=True, stop=True)
        bias = const.tile([P, BOTH], F32, name="bias")
        nc.vector.tensor_copy(out=bias[:], in_=bias_sums[:, 0:BOTH])

        for c in range(1, CHUNKS):
            if c - 1 + AHEAD < CHUNKS:
                load_chunk(c - 1 + AHEAD)
            if c > 1:
                quantise_chunk(c - 1)
                add_bias_pair(c - 2, 0)
            turn_chunk(c)
            if c > 1:
                add_bias_pair(c - 2, 1)
            multiply_chunk(c - 1)
            if c + 1 < CHUNKS:
                for j in SORTED[(c + 1) % 2]:
                    sort_words(c + 1, j)
            if c > 2:
                finish_chunk(c - 3, nc.gpsimd, grouped_tiles[c - 1][:].bitcast(F32)[:, 0 : TILES * QD])

        last = CHUNKS - 1
        kv_before = const.tile([P, TILES * QD], F32, name="kv_before")
        kv_next = const.tile([P, TILES * QD], F32, name="kv_next")
        kv_last = const.tile([P, TILES * QD], F32, name="kv_last")
        quantise_pair(last, 0)
        add_bias_pair(last - 1, 0)
        finish_chunk(last - 2, nc.gpsimd, kv_before[:])
        add_bias_pair(last - 1, 1)
        quantise_pair(last, 1)
        multiply_chunk(last)
        finish_chunk(last - 1, nc.gpsimd, kv_next[:])
        for h in range(PAIRS):
            add_bias_pair(last, h)
        finish_chunk(last, nc.vector, kv_last[:], pieces=PAIRS)
